import numpy as np
import ml_dtypes


def mxq(x, axis, fmt="e4m3"):
    dtype, down = {"e4m3": (ml_dtypes.float8_e4m3fn, 7), "e5m2": (ml_dtypes.float8_e5m2, 14)}[fmt]
    v = np.moveaxis(np.asarray(x, np.float32).astype(ml_dtypes.bfloat16).astype(np.float64), axis, -1)
    blocks = v.reshape(v.shape[:-1] + (-1, 32))
    amax = np.abs(blocks).max(-1, keepdims=True)
    byte = np.maximum(np.where(amax > 0, np.frexp(amax)[1] - 1 + 127, 0) - down, 1)
    scale = np.exp2(byte - 127.0)
    codes = (blocks / scale).astype(np.float32).astype(dtype).astype(np.float64)
    return np.moveaxis((codes * scale).reshape(v.shape), -1, axis)


WIDE = False


def mx_kscale(k):
    if not WIDE:
        return np.ones(k)
    levels = np.array([10, -10, 5, -5, 0])
    a = np.random.permutation(np.resize(levels, k // 512 * 4)).reshape(k // 512, 4)
    idx = np.arange(k)
    return np.exp2(a[idx // 512, idx % 128 // 32])


BF16 = ml_dtypes.bfloat16


def bf(x):
    return np.asarray(x, np.float32).astype(BF16)


def f64(x):
    return np.asarray(x).astype(np.float64)


E2M1 = np.array([0.0, 0.5, 1.0, 1.5, 2.0, 3.0, 4.0, 6.0, -0.0, -0.5, -1.0, -1.5, -2.0, -3.0, -4.0, -6.0])


def pack_weight(w, fmt):
    k, n = w.shape
    w = f64(bf(w)).reshape(k // 32, 32, n)
    amax = np.abs(w).max(1)
    if fmt == "e4m3":
        byte = np.frexp(amax)[1] - 1 + 127 - 7
    else:
        mant, ex = np.frexp(amax / 6.0)
        byte = np.where(mant > 0.5, ex, ex - 1) + 127
    byte = np.clip(np.where(amax > 0, byte, 1), 1, 254)
    scaled = (w * np.exp2(127.0 - byte)[:, None, :]).reshape(k, n).astype(np.float32)
    by_word = np.ascontiguousarray(scaled.reshape(k // 512, 128, 4, n).transpose(0, 1, 3, 2))
    if fmt == "e4m3":
        words = by_word.astype(ml_dtypes.float8_e4m3fn).view(np.uint8)
    else:
        c = by_word.astype(ml_dtypes.float4_e2m1fn).view(np.uint8) & 0xF
        words = c[..., 0::2] | (c[..., 1::2] << 4)
    return np.ascontiguousarray(words), np.ascontiguousarray(byte.astype(np.uint8).reshape(k // 512, 16, n))


def unpack_weight(words, scales, fmt):
    g, p, n, _ = words.shape
    if fmt == "e4m3":
        vals = np.ascontiguousarray(words).view(ml_dtypes.float8_e4m3fn).astype(np.float64)
    else:
        nib = np.empty((g, p, n, 4), np.uint8)
        nib[..., 0::2] = words & 0xF
        nib[..., 1::2] = words >> 4
        vals = E2M1[nib]
    vals = vals * np.repeat(np.exp2(scales.astype(np.float64) - 127.0), 8, axis=1)[..., None]
    return vals.transpose(0, 1, 3, 2).reshape(g * 512, n)

def pack4(w):
    words, scales = pack_weight(w, "e2m1")
    return words.reshape(words.shape[0], 128, -1), scales


def unpack4(words, scales):
    return unpack_weight(words.reshape(words.shape[0], 128, -1, 2), scales, "e2m1")


B, S, C, H, D = 8, 1024, 512, 2, 128
E = H * D


def rope_tables():
    inv_freq = 1.0 / (10000.0 ** (np.arange(0, D, 2) / D))
    emb = np.repeat(np.outer(np.arange(S), inv_freq), 2, axis=1)
    return np.cos(emb), np.sin(emb)


def rope(t, cos, sin):
    tr = t[..., 0::2]
    ti = t[..., 1::2]
    t_rot = np.stack([-ti, tr], axis=-1).reshape(t.shape)
    return t * cos + t_rot * sin


def setup_inputs():
    s = mx_kscale(C)
    cos, sin = rope_tables()
    x = bf(np.random.standard_normal((B, S, C)) * s)
    Wq = np.random.standard_normal((E, C)) / np.sqrt(C) / s[None, :]
    Wq_words, Wq_scales = pack4(np.ascontiguousarray(Wq.T))
    bq = bf(np.random.standard_normal(E) * 0.1)
    return {"x": x,
            "cos": bf(cos), "sin": bf(sin),
            "Wq_words": Wq_words, "Wq_scales": Wq_scales,
            "bq": bq}


def reference(x, cos, sin, Wq_words, Wq_scales, bq):
    y = (mxq(f64(x), 2, "e4m3") @ unpack4(Wq_words, Wq_scales)) + f64(bq)
    q = y.reshape(B, S, H, D).transpose(0, 2, 1, 3)
    return np.maximum(rope(q, f64(cos), f64(sin)), 0.0)

@@ -1,0 +1,220 @@
+from contextlib import ExitStack
+
+import concourse.mybir as mybir
+from concourse.masks import make_identity
+
+F32 = mybir.dt.float32
+BF16 = mybir.dt.bfloat16
+I32 = mybir.dt.int32
+U32 = mybir.dt.uint32
+U8 = mybir.dt.uint8
+FP8X4 = mybir.dt.float8_e4m3fn_x4
+FP4X4 = mybir.dt.float4_e2m1fn_x4
+
+P = 128
+BATCH, TOKENS, K = 8, 1024, 512
+HEADS, HEAD_DIM = 2, 128
+PAIRS = HEAD_DIM // 2
+TOKENS_PER_PARTITION = TOKENS // P
+UNIT_TILES = 4
+UNITS_PER_BATCH = TOKENS_PER_PARTITION // UNIT_TILES
+BANK_TILES = 2
+UNIT_BANKS = UNIT_TILES // BANK_TILES
+UNIT_TOKENS = UNIT_TILES * P
+UNIT_PAIRS = UNIT_TILES * PAIRS
+WORDS = K // 2
+
+FLOPS = 2 * BATCH * TOKENS * K * HEADS * HEAD_DIM
+
+
+def tile_lineartransformerblock_pa_t_kernel(tc, x, cos, sin, Wq_words, Wq_scales, bq, out):
+    nc = tc.nc
+    units = [(b, r) for b in range(BATCH) for r in range(UNITS_PER_BATCH)]
+
+    x_view = x.rearrange("b (p t) k -> b p t k", t=TOKENS_PER_PARTITION)
+    out_view = out.rearrange("b h (p t) d -> b p h (t d)", t=TOKENS_PER_PARTITION)
+
+    with ExitStack() as ctx:
+        ctx.enter_context(tc.manual_schedule())
+        consts = ctx.enter_context(tc.tile_pool(name="consts", bufs=1))
+        x_pool = ctx.enter_context(tc.tile_pool(name="x", bufs=len(units) * UNIT_BANKS))
+        work = ctx.enter_context(tc.tile_pool(name="work", bufs=4))
+        out_pool = ctx.enter_context(tc.tile_pool(name="out", bufs=12))
+        xt_pool = ctx.enter_context(tc.psum_pool(name="xt", bufs=4))
+        y_pool = ctx.enter_context(tc.psum_pool(name="y", bufs=4))
+
+        def load_x(u):
+            b, r = units[u]
+            pieces = []
+            for bank in range(UNIT_BANKS):
+                first = r * UNIT_TILES + bank * BANK_TILES
+                x_sb = x_pool.tile([P, BANK_TILES, K], BF16)
+                nc.sync.dma_start(out=x_sb[:], in_=x_view[b, :, first : first + BANK_TILES, :])
+                pieces.append(x_sb)
+            return pieces
+
+        x_tiles = [load_x(0), load_x(1)]
+
+        w_words = consts.tile([P, 2 * HEADS * HEAD_DIM], U8, align_bytes=64)
+        nc.sync.dma_start(out=w_words[:].bitcast(I32), in_=Wq_words[0].bitcast(I32))
+        w_scales = consts.tile([P, HEADS * HEAD_DIM], U8, align_bytes=64)
+        nc.vector.memset(w_scales[:].bitcast(I32), 0)
+        for quadrant in range(4):
+            nc.sync.dma_start(
+                out=w_scales[32 * quadrant : 32 * quadrant + 4, :].bitcast(I32),
+                in_=Wq_scales[0, 4 * quadrant : 4 * quadrant + 4, :].bitcast(I32),
+            )
+        for u in range(2, len(units)):
+            x_tiles.append(load_x(u))
+
+        identity = consts.tile([P, P], F32)
+        make_identity(nc, identity[:])
+
+        cos_planes = consts.tile([P, 2, TOKENS_PER_PARTITION * PAIRS], F32)
+        sin_planes = consts.tile([P, 2, TOKENS_PER_PARTITION * PAIRS], F32)
+        cos_raw = consts.tile([P, TOKENS_PER_PARTITION, HEAD_DIM], BF16)
+        sin_raw = consts.tile([P, TOKENS_PER_PARTITION, HEAD_DIM], BF16)
+        for raw, table in ((cos_raw, cos), (sin_raw, sin)):
+            nc.gpsimd.dma_start(out=raw[:], in_=table.rearrange("(p t) d -> p t d", t=TOKENS_PER_PARTITION))
+        for j in range(2):
+            for planes, raw, sign in ((cos_planes, cos_raw, 1.0), (sin_planes, sin_raw, 2.0 * j - 1.0)):
+                nc.gpsimd.tensor_scalar(
+                    out=planes[:, j, :].rearrange("p (t i) -> p t i", i=PAIRS),
+                    in0=raw[:, :, j:HEAD_DIM:2],
+                    scalar1=sign,
+                    scalar2=0.0,
+                    op0=mybir.AluOpType.mult,
+                    op1=mybir.AluOpType.add,
+                )
+
+        table_warmer = consts.tile([P, 1], F32)
+        nc.vector.memset(table_warmer[:], 0.0)
+        nc.scalar.activation(out=table_warmer[:], in_=table_warmer[:], func=mybir.ActivationFunctionType.Relu)
+
+        bias_rows = consts.tile([P, HEADS * HEAD_DIM], BF16)
+        nc.vector.memset(bias_rows[:], 0.0)
+        nc.scalar.dma_start(out=bias_rows[0:1, :], in_=bq.unsqueeze(0))
+        ones = consts.tile([P, P], BF16)
+        nc.vector.memset(ones[:], 1.0)
+
+        grouped_of, codes_of, y_of, turned_of, crossed_of = {}, {}, {}, {}, {}
+
+        def transpose_and_regroup(u):
+            grouped = work.tile([P, 4 * UNIT_TOKENS], BF16, align_bytes=64)
+            grouped_words = grouped[:].bitcast(F32).rearrange("p (c half) -> p c half", half=2)
+            for bank in range(UNIT_BANKS):
+                x_words = x_tiles[u][bank][:].bitcast(F32)
+                xt = xt_pool.tile([P, 2, BANK_TILES * P], F32)
+                for i in range(BANK_TILES):
+                    for half in range(2):
+                        nc.tensor.transpose(
+                            out=xt[:, half, i * P : (i + 1) * P],
+                            in_=x_words[:, i, half:WORDS:2],
+                            identity=identity[:],
+                        )
+                nc.scalar.copy(
+                    out=grouped_words[:, bank * BANK_TILES * P : (bank + 1) * BANK_TILES * P, :],
+                    in_=xt[:].rearrange("p half c -> p c half"),
+                )
+            grouped_of[u] = grouped
+
+        def quantise(u):
+            codes = work.tile([P, UNIT_TOKENS], U32, align_bytes=64)
+            scales = work.tile([P, UNIT_TOKENS], U8, align_bytes=64)
+            nc.vector.quantize_mx(out=codes[:].bitcast(FP8X4), scales=scales[:], in_=grouped_of[u][:])
+            codes_of[u] = (codes, scales)
+
+        def multiply(u):
+            codes, scales = codes_of[u]
+            y_heads = []
+            for h in range(HEADS):
+                y = y_pool.tile([P, UNIT_TILES * HEAD_DIM], F32)
+                y_heads.append(y)
+            for i in range(UNIT_TILES):
+                for h in range(HEADS):
+                    nc.tensor.matmul_mx(
+                        out=y_heads[h][:, i * HEAD_DIM : (i + 1) * HEAD_DIM],
+                        lhsT=codes[:, i * P : (i + 1) * P].bitcast(FP8X4),
+                        lhsT_scale=scales[:, i * P : (i + 1) * P],
+                        rhs=w_words[:, 2 * h * HEAD_DIM : 2 * (h + 1) * HEAD_DIM].bitcast(FP4X4),
+                        rhs_scale=w_scales[:, h * HEAD_DIM : (h + 1) * HEAD_DIM],
+                        start=True,
+                        stop=True,
+                    )
+            y_of[u] = y_heads
+
+        def add_bias(u):
+            turned = work.tile([P, HEADS, 2, UNIT_PAIRS], F32)
+            for h, y in enumerate(y_of[u]):
+                nc.vector.tensor_tensor(
+                    out=turned[:, h, :, :].rearrange("p j (t i) -> p j t i", i=PAIRS),
+                    in0=y[:].rearrange("p (t i j) -> p j t i", i=PAIRS, j=2),
+                    in1=bias[:, h, :, :].unsqueeze(2).to_broadcast([P, 2, UNIT_TILES, PAIRS]),
+                    op=mybir.AluOpType.add,
+                )
+            turned_of[u] = turned
+
+        def multiply_by_tables(u):
+            r = units[u][1]
+            turned = turned_of[u]
+            mine = slice(r * UNIT_PAIRS, (r + 1) * UNIT_PAIRS)
+            crossed = work.tile([P, HEADS, 2, UNIT_PAIRS], F32)
+            for j in range(2):
+                nc.vector.tensor_tensor(
+                    out=crossed[:, :, j, :],
+                    in0=turned[:, :, 1 - j, :],
+                    in1=sin_planes[:, j, mine].unsqueeze(1).to_broadcast([P, HEADS, UNIT_PAIRS]),
+                    op=mybir.AluOpType.mult,
+                )
+            nc.vector.tensor_tensor(
+                out=turned[:],
+                in0=turned[:],
+                in1=cos_planes[:, :, mine].unsqueeze(1).to_broadcast([P, HEADS, 2, UNIT_PAIRS]),
+                op=mybir.AluOpType.mult,
+            )
+            crossed_of[u] = crossed
+
+        def add_products(u):
+            turned = turned_of[u]
+            nc.vector.tensor_tensor(out=turned[:], in0=turned[:], in1=crossed_of[u][:], op=mybir.AluOpType.add)
+
+        def relu_and_store(u):
+            b, r = units[u]
+            run = UNIT_TILES * HEAD_DIM
+            for h in range(HEADS):
+                result = out_pool.tile([P, UNIT_PAIRS, 2], F32)
+                planes = turned_of[u][:, h, :, :].rearrange("p j c -> p c j")
+                if u == len(units) - 1 and h == HEADS - 1:
+                    nc.vector.tensor_scalar_max(out=result[:], in0=planes, scalar1=0.0)
+                else:
+                    nc.scalar.activation(out=result[:], in_=planes, func=mybir.ActivationFunctionType.Relu)
+                nc.sync.dma_start(
+                    out=out_view[b, :, h, r * run : (r + 1) * run],
+                    in_=result[:].rearrange("p c j -> p (c j)"),
+                )
+
+        transpose_and_regroup(0)
+
+        bias_bank = y_pool.tile([P, UNIT_TILES * HEAD_DIM], F32, tag="y")
+        bias_spread = bias_bank[:, 0 : HEADS * HEAD_DIM]
+        nc.tensor.matmul(out=bias_spread, lhsT=ones[:], rhs=bias_rows[:], start=True, stop=True)
+        bias = consts.tile([P, HEADS, 2, PAIRS], F32)
+        nc.vector.tensor_copy(out=bias[:], in_=bias_spread.rearrange("p (h i j) -> p h j i", h=HEADS, j=2))
+
+        def in_range(u):
+            return 0 <= u < len(units)
+
+        for step in range(1, len(units) + 4):
+            if in_range(step):
+                transpose_and_regroup(step)
+            if in_range(step - 1):
+                quantise(step - 1)
+                multiply(step - 1)
+            if in_range(step - 3):
+                multiply_by_tables(step - 3)
+            if in_range(step - 2):
+                add_bias(step - 2)
+            if in_range(step - 3):
+                add_products(step - 3)
+            if in_range(step - 4):
+                relu_and_store(step - 4)

@@ -21,7 +21,6 @@ UNITS_PER_BATCH = TOKENS_PER_PARTITION // UNIT_TILES
 BANK_TILES = 2
 UNIT_BANKS = UNIT_TILES // BANK_TILES
 UNIT_TOKENS = UNIT_TILES * P
-UNIT_PAIRS = UNIT_TILES * PAIRS
 WORDS = K // 2
 
 FLOPS = 2 * BATCH * TOKENS * K * HEADS * HEAD_DIM
@@ -39,9 +38,10 @@ def tile_lineartransformerblock_pa_t_kernel(tc, x, cos, sin, Wq_words, Wq_scales
         consts = ctx.enter_context(tc.tile_pool(name="consts", bufs=1))
         x_pool = ctx.enter_context(tc.tile_pool(name="x", bufs=len(units) * UNIT_BANKS))
         work = ctx.enter_context(tc.tile_pool(name="work", bufs=4))
-        out_pool = ctx.enter_context(tc.tile_pool(name="out", bufs=12))
-        xt_pool = ctx.enter_context(tc.psum_pool(name="xt", bufs=4))
+        out_pool = ctx.enter_context(tc.tile_pool(name="out", bufs=8))
+        xt_pool = ctx.enter_context(tc.psum_pool(name="xt", bufs=2))
         y_pool = ctx.enter_context(tc.psum_pool(name="y", bufs=4))
+        bt_pool = ctx.enter_context(tc.psum_pool(name="bt", bufs=2))
 
         def load_x(u):
             b, r = units[u]
@@ -69,35 +69,37 @@ def tile_lineartransformerblock_pa_t_kernel(tc, x, cos, sin, Wq_words, Wq_scales
 
         identity = consts.tile([P, P], F32)
         make_identity(nc, identity[:])
+        identity_bf = consts.tile([P, P], BF16)
+        make_identity(nc, identity_bf[:])
+        swap = consts.tile([P, PAIRS, 2], F32)
+        identity_pairs = identity[:].rearrange("p (i j) -> p i j", j=2)
+        for j in range(2):
+            nc.gpsimd.tensor_copy(out=swap[:, :, j], in_=identity_pairs[:, :, 1 - j])
 
-        cos_planes = consts.tile([P, 2, TOKENS_PER_PARTITION * PAIRS], F32)
-        sin_planes = consts.tile([P, 2, TOKENS_PER_PARTITION * PAIRS], F32)
         cos_raw = consts.tile([P, TOKENS_PER_PARTITION, HEAD_DIM], BF16)
         sin_raw = consts.tile([P, TOKENS_PER_PARTITION, HEAD_DIM], BF16)
-        for raw, table in ((cos_raw, cos), (sin_raw, sin)):
-            nc.gpsimd.dma_start(out=raw[:], in_=table.rearrange("(p t) d -> p t d", t=TOKENS_PER_PARTITION))
-        for j in range(2):
-            for planes, raw, sign in ((cos_planes, cos_raw, 1.0), (sin_planes, sin_raw, 2.0 * j - 1.0)):
-                nc.gpsimd.tensor_scalar(
-                    out=planes[:, j, :].rearrange("p (t i) -> p t i", i=PAIRS),
-                    in0=raw[:, :, j:HEAD_DIM:2],
-                    scalar1=sign,
-                    scalar2=0.0,
-                    op0=mybir.AluOpType.mult,
-                    op1=mybir.AluOpType.add,
-                )
+        for raw, table in ((sin_raw, sin), (cos_raw, cos)):
+            nc.scalar.dma_start(out=raw[:], in_=table.rearrange("(p t) d -> p t d", t=TOKENS_PER_PARTITION))
 
         table_warmer = consts.tile([P, 1], F32)
         nc.vector.memset(table_warmer[:], 0.0)
         nc.scalar.activation(out=table_warmer[:], in_=table_warmer[:], func=mybir.ActivationFunctionType.Relu)
 
-        bias_rows = consts.tile([P, HEADS * HEAD_DIM], BF16)
+        bias_rows = consts.tile([P, HEAD_DIM], BF16)
         nc.vector.memset(bias_rows[:], 0.0)
-        nc.scalar.dma_start(out=bias_rows[0:1, :], in_=bq.unsqueeze(0))
-        ones = consts.tile([P, P], BF16)
-        nc.vector.memset(ones[:], 1.0)
+        nc.scalar.dma_start(out=bias_rows[0:HEADS, :], in_=bq.rearrange("(h d) -> h d", h=HEADS))
 
-        grouped_of, codes_of, y_of, turned_of, crossed_of = {}, {}, {}, {}, {}
+        partner_sin = consts.tile([P, TOKENS_PER_PARTITION, HEAD_DIM], BF16)
+        for j in range(2):
+            nc.vector.tensor_scalar(
+                out=partner_sin[:, :, j:HEAD_DIM:2],
+                in0=sin_raw[:, :, 1 - j : HEAD_DIM : 2],
+                scalar1=1.0 - 2.0 * j,
+                scalar2=None,
+                op0=mybir.AluOpType.mult,
+            )
+
+        grouped_of, codes_of, y_of, prod_of, bt_of = {}, {}, {}, {}, {}
 
         def transpose_and_regroup(u):
             grouped = work.tile([P, 4 * UNIT_TOKENS], BF16, align_bytes=64)
@@ -128,93 +130,89 @@ def tile_lineartransformerblock_pa_t_kernel(tc, x, cos, sin, Wq_words, Wq_scales
             codes, scales = codes_of[u]
             y_heads = []
             for h in range(HEADS):
-                y = y_pool.tile([P, UNIT_TILES * HEAD_DIM], F32)
-                y_heads.append(y)
-            for i in range(UNIT_TILES):
-                for h in range(HEADS):
-                    nc.tensor.matmul_mx(
-                        out=y_heads[h][:, i * HEAD_DIM : (i + 1) * HEAD_DIM],
-                        lhsT=codes[:, i * P : (i + 1) * P].bitcast(FP8X4),
-                        lhsT_scale=scales[:, i * P : (i + 1) * P],
-                        rhs=w_words[:, 2 * h * HEAD_DIM : 2 * (h + 1) * HEAD_DIM].bitcast(FP4X4),
-                        rhs_scale=w_scales[:, h * HEAD_DIM : (h + 1) * HEAD_DIM],
-                        start=True,
-                        stop=True,
-                    )
-            y_of[u] = y_heads
-
-        def add_bias(u):
-            turned = work.tile([P, HEADS, 2, UNIT_PAIRS], F32)
-            for h, y in enumerate(y_of[u]):
-                nc.vector.tensor_tensor(
-                    out=turned[:, h, :, :].rearrange("p j (t i) -> p j t i", i=PAIRS),
-                    in0=y[:].rearrange("p (t i j) -> p j t i", i=PAIRS, j=2),
-                    in1=bias[:, h, :, :].unsqueeze(2).to_broadcast([P, 2, UNIT_TILES, PAIRS]),
-                    op=mybir.AluOpType.add,
+                y = y_pool.tile([P, UNIT_TOKENS], F32)
+                nc.tensor.matmul_mx(
+                    out=y[:],
+                    lhsT=w_words[:, 2 * h * HEAD_DIM : 2 * (h + 1) * HEAD_DIM].bitcast(FP4X4),
+                    lhsT_scale=w_scales[:, h * HEAD_DIM : (h + 1) * HEAD_DIM],
+                    rhs=codes[:].bitcast(FP8X4),
+                    rhs_scale=scales[:],
+                    start=True,
+                    stop=True,
                 )
-            turned_of[u] = turned
+                y_heads.append(y)
+            y_of[u] = y_heads
 
         def multiply_by_tables(u):
             r = units[u][1]
-            turned = turned_of[u]
-            mine = slice(r * UNIT_PAIRS, (r + 1) * UNIT_PAIRS)
-            crossed = work.tile([P, HEADS, 2, UNIT_PAIRS], F32)
-            for j in range(2):
-                nc.vector.tensor_tensor(
-                    out=crossed[:, :, j, :],
-                    in0=turned[:, :, 1 - j, :],
-                    in1=sin_planes[:, j, mine].unsqueeze(1).to_broadcast([P, HEADS, UNIT_PAIRS]),
-                    op=mybir.AluOpType.mult,
+            mine = slice(r * UNIT_TOKENS, (r + 1) * UNIT_TOKENS)
+            prods = []
+            for h, y in enumerate(y_of[u]):
+                prod = work.tile([P, 2, UNIT_TOKENS], F32)
+                nc.vector.scalar_tensor_tensor(
+                    out=prod[:],
+                    in0=y[:].unsqueeze(1).to_broadcast([P, 2, UNIT_TOKENS]),
+                    scalar=bias[:, h : h + 1],
+                    in1=tables[:, :, mine],
+                    op0=mybir.AluOpType.add,
+                    op1=mybir.AluOpType.mult,
                 )
-            nc.vector.tensor_tensor(
-                out=turned[:],
-                in0=turned[:],
-                in1=cos_planes[:, :, mine].unsqueeze(1).to_broadcast([P, HEADS, 2, UNIT_PAIRS]),
-                op=mybir.AluOpType.mult,
-            )
-            crossed_of[u] = crossed
+                prods.append(prod)
+            prod_of[u] = prods
 
-        def add_products(u):
-            turned = turned_of[u]
-            nc.vector.tensor_tensor(out=turned[:], in0=turned[:], in1=crossed_of[u][:], op=mybir.AluOpType.add)
+        def turn_back(u):
+            banks = []
+            for h in range(HEADS):
+                prod = prod_of[u][h]
+                bt = bt_pool.tile([P, UNIT_TILES * HEAD_DIM], F32)
+                for i in range(UNIT_TILES):
+                    cols = slice(i * P, (i + 1) * P)
+                    nc.tensor.matmul(
+                        out=bt[:, cols], lhsT=prod[:, 0, cols], rhs=identity[:], is_transpose=True, start=True, stop=False
+                    )
+                    nc.tensor.matmul(
+                        out=bt[:, cols],
+                        lhsT=prod[:, 1, cols],
+                        rhs=swap[:].rearrange("p i j -> p (i j)"),
+                        is_transpose=True,
+                        start=False,
+                        stop=True,
+                    )
+                banks.append(bt)
+            bt_of[u] = banks
 
         def relu_and_store(u):
             b, r = units[u]
             run = UNIT_TILES * HEAD_DIM
             for h in range(HEADS):
-                result = out_pool.tile([P, UNIT_PAIRS, 2], F32)
-                planes = turned_of[u][:, h, :, :].rearrange("p j c -> p c j")
-                if u == len(units) - 1 and h == HEADS - 1:
-                    nc.vector.tensor_scalar_max(out=result[:], in0=planes, scalar1=0.0)
-                else:
-                    nc.scalar.activation(out=result[:], in_=planes, func=mybir.ActivationFunctionType.Relu)
-                nc.sync.dma_start(
-                    out=out_view[b, :, h, r * run : (r + 1) * run],
-                    in_=result[:].rearrange("p c j -> p (c j)"),
-                )
+                result = out_pool.tile([P, run], F32)
+                nc.scalar.activation(out=result[:], in_=bt_of[u][h][:], func=mybir.ActivationFunctionType.Relu)
+                nc.sync.dma_start(out=out_view[b, :, h, r * run : (r + 1) * run], in_=result[:])
 
         transpose_and_regroup(0)
 
-        bias_bank = y_pool.tile([P, UNIT_TILES * HEAD_DIM], F32, tag="y")
-        bias_spread = bias_bank[:, 0 : HEADS * HEAD_DIM]
-        nc.tensor.matmul(out=bias_spread, lhsT=ones[:], rhs=bias_rows[:], start=True, stop=True)
-        bias = consts.tile([P, HEADS, 2, PAIRS], F32)
-        nc.vector.tensor_copy(out=bias[:], in_=bias_spread.rearrange("p (h i j) -> p h j i", h=HEADS, j=2))
+        tables = consts.tile([P, 2, TOKENS], BF16)
+        for which, raw in enumerate((cos_raw, partner_sin)):
+            turned = y_pool.tile([P, TOKENS], BF16, tag="y")
+            for t in range(TOKENS_PER_PARTITION):
+                nc.tensor.transpose(out=turned[:, t * P : (t + 1) * P], in_=raw[:, t, :], identity=identity_bf[:])
+            nc.vector.tensor_copy(out=tables[:, which, :], in_=turned[:])
+        bias_turned = y_pool.tile([P, P], BF16, tag="y")
+        nc.tensor.transpose(out=bias_turned[:], in_=bias_rows[:], identity=identity_bf[:])
+        bias = consts.tile([P, HEADS], F32)
+        nc.vector.tensor_copy(out=bias[:], in_=bias_turned[:, 0:HEADS])
 
         def in_range(u):
             return 0 <= u < len(units)
 
-        for step in range(1, len(units) + 4):
+        for step in range(1, len(units) + 3):
+            if in_range(step - 3):
+                relu_and_store(step - 3)
             if in_range(step):
                 transpose_and_regroup(step)
             if in_range(step - 1):
                 quantise(step - 1)
                 multiply(step - 1)
-            if in_range(step - 3):
-                multiply_by_tables(step - 3)
             if in_range(step - 2):
-                add_bias(step - 2)
-            if in_range(step - 3):
-                add_products(step - 3)
-            if in_range(step - 4):
-                relu_and_store(step - 4)
+                multiply_by_tables(step - 2)
+                turn_back(step - 2)

@@ -38,6 +38,7 @@ def tile_lineartransformerblock_pa_t_kernel(tc, x, cos, sin, Wq_words, Wq_scales
         consts = ctx.enter_context(tc.tile_pool(name="consts", bufs=1))
         x_pool = ctx.enter_context(tc.tile_pool(name="x", bufs=len(units) * UNIT_BANKS))
         work = ctx.enter_context(tc.tile_pool(name="work", bufs=4))
+        prod_pool = ctx.enter_context(tc.tile_pool(name="prod", bufs=6))
         out_pool = ctx.enter_context(tc.tile_pool(name="out", bufs=8))
         xt_pool = ctx.enter_context(tc.psum_pool(name="xt", bufs=2))
         y_pool = ctx.enter_context(tc.psum_pool(name="y", bufs=4))
@@ -99,26 +100,26 @@ def tile_lineartransformerblock_pa_t_kernel(tc, x, cos, sin, Wq_words, Wq_scales
                 op0=mybir.AluOpType.mult,
             )
 
-        grouped_of, codes_of, y_of, prod_of, bt_of = {}, {}, {}, {}, {}
+        grouped_of, codes_of, y_of, prod_of = {}, {}, {}, {}
 
-        def transpose_and_regroup(u):
-            grouped = work.tile([P, 4 * UNIT_TOKENS], BF16, align_bytes=64)
-            grouped_words = grouped[:].bitcast(F32).rearrange("p (c half) -> p c half", half=2)
-            for bank in range(UNIT_BANKS):
-                x_words = x_tiles[u][bank][:].bitcast(F32)
-                xt = xt_pool.tile([P, 2, BANK_TILES * P], F32)
-                for i in range(BANK_TILES):
-                    for half in range(2):
-                        nc.tensor.transpose(
-                            out=xt[:, half, i * P : (i + 1) * P],
-                            in_=x_words[:, i, half:WORDS:2],
-                            identity=identity[:],
-                        )
-                nc.scalar.copy(
-                    out=grouped_words[:, bank * BANK_TILES * P : (bank + 1) * BANK_TILES * P, :],
-                    in_=xt[:].rearrange("p half c -> p c half"),
-                )
-            grouped_of[u] = grouped
+        def transpose_and_regroup(u, bank):
+            if bank == 0:
+                grouped = work.tile([P, 4 * UNIT_TOKENS], BF16, align_bytes=64)
+                grouped_of[u] = grouped
+            grouped_words = grouped_of[u][:].bitcast(F32).rearrange("p (c half) -> p c half", half=2)
+            x_words = x_tiles[u][bank][:].bitcast(F32)
+            xt = xt_pool.tile([P, 2, BANK_TILES * P], F32)
+            for i in range(BANK_TILES):
+                for half in range(2):
+                    nc.tensor.transpose(
+                        out=xt[:, half, i * P : (i + 1) * P],
+                        in_=x_words[:, i, half:WORDS:2],
+                        identity=identity[:],
+                    )
+            nc.scalar.copy(
+                out=grouped_words[:, bank * BANK_TILES * P : (bank + 1) * BANK_TILES * P, :],
+                in_=xt[:].rearrange("p half c -> p c half"),
+            )
 
         def quantise(u):
             codes = work.tile([P, UNIT_TOKENS], U32, align_bytes=64)
@@ -148,7 +149,7 @@ def tile_lineartransformerblock_pa_t_kernel(tc, x, cos, sin, Wq_words, Wq_scales
             mine = slice(r * UNIT_TOKENS, (r + 1) * UNIT_TOKENS)
             prods = []
             for h, y in enumerate(y_of[u]):
-                prod = work.tile([P, 2, UNIT_TOKENS], F32)
+                prod = prod_pool.tile([P, 2, UNIT_TOKENS], F32)
                 nc.vector.scalar_tensor_tensor(
                     out=prod[:],
                     in0=y[:].unsqueeze(1).to_broadcast([P, 2, UNIT_TOKENS]),
@@ -160,36 +161,30 @@ def tile_lineartransformerblock_pa_t_kernel(tc, x, cos, sin, Wq_words, Wq_scales
                 prods.append(prod)
             prod_of[u] = prods
 
-        def turn_back(u):
-            banks = []
-            for h in range(HEADS):
-                prod = prod_of[u][h]
-                bt = bt_pool.tile([P, UNIT_TILES * HEAD_DIM], F32)
-                for i in range(UNIT_TILES):
-                    cols = slice(i * P, (i + 1) * P)
-                    nc.tensor.matmul(
-                        out=bt[:, cols], lhsT=prod[:, 0, cols], rhs=identity[:], is_transpose=True, start=True, stop=False
-                    )
-                    nc.tensor.matmul(
-                        out=bt[:, cols],
-                        lhsT=prod[:, 1, cols],
-                        rhs=swap[:].rearrange("p i j -> p (i j)"),
-                        is_transpose=True,
-                        start=False,
-                        stop=True,
-                    )
-                banks.append(bt)
-            bt_of[u] = banks
-
-        def relu_and_store(u):
+        def turn_back_relu_store(u, h):
             b, r = units[u]
             run = UNIT_TILES * HEAD_DIM
-            for h in range(HEADS):
-                result = out_pool.tile([P, run], F32)
-                nc.scalar.activation(out=result[:], in_=bt_of[u][h][:], func=mybir.ActivationFunctionType.Relu)
-                nc.sync.dma_start(out=out_view[b, :, h, r * run : (r + 1) * run], in_=result[:])
+            prod = prod_of[u][h]
+            bt = bt_pool.tile([P, run], F32)
+            for i in range(UNIT_TILES):
+                cols = slice(i * P, (i + 1) * P)
+                nc.tensor.matmul(
+                    out=bt[:, cols], lhsT=prod[:, 0, cols], rhs=identity[:], is_transpose=True, start=True, stop=False
+                )
+                nc.tensor.matmul(
+                    out=bt[:, cols],
+                    lhsT=prod[:, 1, cols],
+                    rhs=swap[:].rearrange("p i j -> p (i j)"),
+                    is_transpose=True,
+                    start=False,
+                    stop=True,
+                )
+            result = out_pool.tile([P, run], F32)
+            nc.scalar.activation(out=result[:], in_=bt[:], func=mybir.ActivationFunctionType.Relu)
+            nc.sync.dma_start(out=out_view[b, :, h, r * run : (r + 1) * run], in_=result[:])
 
-        transpose_and_regroup(0)
+        for bank in range(UNIT_BANKS):
+            transpose_and_regroup(0, bank)
 
         tables = consts.tile([P, 2, TOKENS], BF16)
         for which, raw in enumerate((cos_raw, partner_sin)):
@@ -205,14 +200,14 @@ def tile_lineartransformerblock_pa_t_kernel(tc, x, cos, sin, Wq_words, Wq_scales
         def in_range(u):
             return 0 <= u < len(units)
 
-        for step in range(1, len(units) + 3):
-            if in_range(step - 3):
-                relu_and_store(step - 3)
-            if in_range(step):
-                transpose_and_regroup(step)
+        for step in range(1, len(units) + 4):
+            for half_step in range(2):
+                if in_range(step):
+                    transpose_and_regroup(step, half_step)
+                if in_range(step - 3):
+                    turn_back_relu_store(step - 3, half_step)
             if in_range(step - 1):
                 quantise(step - 1)
                 multiply(step - 1)
             if in_range(step - 2):
                 multiply_by_tables(step - 2)
-                turn_back(step - 2)

@@ -22,6 +22,8 @@ BANK_TILES = 2
 UNIT_BANKS = UNIT_TILES // BANK_TILES
 UNIT_TOKENS = UNIT_TILES * P
 WORDS = K // 2
+SORTED_BANK = 1
+FIRST_SORTED_UNIT = 2
 
 FLOPS = 2 * BATCH * TOKENS * K * HEADS * HEAD_DIM
 
@@ -40,6 +42,7 @@ def tile_lineartransformerblock_pa_t_kernel(tc, x, cos, sin, Wq_words, Wq_scales
         work = ctx.enter_context(tc.tile_pool(name="work", bufs=4))
         prod_pool = ctx.enter_context(tc.tile_pool(name="prod", bufs=6))
         out_pool = ctx.enter_context(tc.tile_pool(name="out", bufs=8))
+        sorted_pool = ctx.enter_context(tc.tile_pool(name="sorted", bufs=3))
         xt_pool = ctx.enter_context(tc.psum_pool(name="xt", bufs=2))
         y_pool = ctx.enter_context(tc.psum_pool(name="y", bufs=4))
         bt_pool = ctx.enter_context(tc.psum_pool(name="bt", bufs=2))
@@ -102,6 +105,16 @@ def tile_lineartransformerblock_pa_t_kernel(tc, x, cos, sin, Wq_words, Wq_scales
 
         grouped_of, codes_of, y_of, prod_of = {}, {}, {}, {}
 
+        sorted_of = {}
+
+        def sort_words(u):
+            x_sorted = sorted_pool.tile([P, BANK_TILES, 2, WORDS // 2], F32)
+            nc.scalar.copy(
+                out=x_sorted[:],
+                in_=x_tiles[u][SORTED_BANK][:].bitcast(F32).rearrange("p i (w half) -> p i half w", half=2),
+            )
+            sorted_of[u] = x_sorted
+
         def transpose_and_regroup(u, bank):
             if bank == 0:
                 grouped = work.tile([P, 4 * UNIT_TOKENS], BF16, align_bytes=64)
@@ -111,11 +124,11 @@ def tile_lineartransformerblock_pa_t_kernel(tc, x, cos, sin, Wq_words, Wq_scales
             xt = xt_pool.tile([P, 2, BANK_TILES * P], F32)
             for i in range(BANK_TILES):
                 for half in range(2):
-                    nc.tensor.transpose(
-                        out=xt[:, half, i * P : (i + 1) * P],
-                        in_=x_words[:, i, half:WORDS:2],
-                        identity=identity[:],
-                    )
+                    if bank == SORTED_BANK and u in sorted_of:
+                        words_in = sorted_of[u][:, i, half, :]
+                    else:
+                        words_in = x_words[:, i, half:WORDS:2]
+                    nc.tensor.transpose(out=xt[:, half, i * P : (i + 1) * P], in_=words_in, identity=identity[:])
             nc.scalar.copy(
                 out=grouped_words[:, bank * BANK_TILES * P : (bank + 1) * BANK_TILES * P, :],
                 in_=xt[:].rearrange("p half c -> p c half"),
@@ -202,6 +215,8 @@ def tile_lineartransformerblock_pa_t_kernel(tc, x, cos, sin, Wq_words, Wq_scales
 
         for step in range(1, len(units) + 4):
             for half_step in range(2):
+                if half_step == 1 and in_range(step + 1) and step + 1 >= FIRST_SORTED_UNIT:
+                    sort_words(step + 1)
                 if in_range(step):
                     transpose_and_regroup(step, half_step)
                 if in_range(step - 3):

@@ -23,7 +23,7 @@ UNIT_BANKS = UNIT_TILES // BANK_TILES
 UNIT_TOKENS = UNIT_TILES * P
 WORDS = K // 2
 SORTED_BANK = 1
-FIRST_SORTED_UNIT = 2
+FIRST_SORTED_UNIT = 3
 
 FLOPS = 2 * BATCH * TOKENS * K * HEADS * HEAD_DIM
 
@@ -57,7 +57,14 @@ def tile_lineartransformerblock_pa_t_kernel(tc, x, cos, sin, Wq_words, Wq_scales
                 pieces.append(x_sb)
             return pieces
 
-        x_tiles = [load_x(0), load_x(1)]
+        x_tiles = [load_x(0)]
+
+        cos_raw = consts.tile([P, TOKENS_PER_PARTITION, HEAD_DIM], BF16)
+        sin_raw = consts.tile([P, TOKENS_PER_PARTITION, HEAD_DIM], BF16)
+        for raw, table in ((sin_raw, sin), (cos_raw, cos)):
+            nc.sync.dma_start(out=raw[:], in_=table.rearrange("(p t) d -> p t d", t=TOKENS_PER_PARTITION))
+
+        x_tiles.append(load_x(1))
 
         w_words = consts.tile([P, 2 * HEADS * HEAD_DIM], U8, align_bytes=64)
         nc.sync.dma_start(out=w_words[:].bitcast(I32), in_=Wq_words[0].bitcast(I32))
@@ -79,11 +86,6 @@ def tile_lineartransformerblock_pa_t_kernel(tc, x, cos, sin, Wq_words, Wq_scales
         identity_pairs = identity[:].rearrange("p (i j) -> p i j", j=2)
         for j in range(2):
             nc.gpsimd.tensor_copy(out=swap[:, :, j], in_=identity_pairs[:, :, 1 - j])
-
-        cos_raw = consts.tile([P, TOKENS_PER_PARTITION, HEAD_DIM], BF16)
-        sin_raw = consts.tile([P, TOKENS_PER_PARTITION, HEAD_DIM], BF16)
-        for raw, table in ((sin_raw, sin), (cos_raw, cos)):
-            nc.scalar.dma_start(out=raw[:], in_=table.rearrange("(p t) d -> p t d", t=TOKENS_PER_PARTITION))
 
         table_warmer = consts.tile([P, 1], F32)
         nc.vector.memset(table_warmer[:], 0.0)
@@ -200,13 +202,17 @@ def tile_lineartransformerblock_pa_t_kernel(tc, x, cos, sin, Wq_words, Wq_scales
             transpose_and_regroup(0, bank)
 
         tables = consts.tile([P, 2, TOKENS], BF16)
-        for which, raw in enumerate((cos_raw, partner_sin)):
+        turned_tables = []
+        for raw in (cos_raw, partner_sin):
             turned = y_pool.tile([P, TOKENS], BF16, tag="y")
             for t in range(TOKENS_PER_PARTITION):
                 nc.tensor.transpose(out=turned[:, t * P : (t + 1) * P], in_=raw[:, t, :], identity=identity_bf[:])
-            nc.vector.tensor_copy(out=tables[:, which, :], in_=turned[:])
+            turned_tables.append(turned)
         bias_turned = y_pool.tile([P, P], BF16, tag="y")
         nc.tensor.transpose(out=bias_turned[:], in_=bias_rows[:], identity=identity_bf[:])
+        quantise(0)
+        for which, turned in enumerate(turned_tables):
+            nc.vector.tensor_copy(out=tables[:, which, :], in_=turned[:])
         bias = consts.tile([P, HEADS], F32)
         nc.vector.tensor_copy(out=bias[:], in_=bias_turned[:, 0:HEADS])
 
@@ -222,7 +228,8 @@ def tile_lineartransformerblock_pa_t_kernel(tc, x, cos, sin, Wq_words, Wq_scales
                 if in_range(step - 3):
                     turn_back_relu_store(step - 3, half_step)
             if in_range(step - 1):
-                quantise(step - 1)
                 multiply(step - 1)
             if in_range(step - 2):
                 multiply_by_tables(step - 2)
+            if in_range(step):
+                quantise(step)

@@ -24,6 +24,8 @@ UNIT_TOKENS = UNIT_TILES * P
 WORDS = K // 2
 SORTED_BANK = 1
 FIRST_SORTED_UNIT = 3
+WARM_UP_MATMULS = 5
+LAST_PIECES = 2
 
 FLOPS = 2 * BATCH * TOKENS * K * HEADS * HEAD_DIM
 
@@ -46,6 +48,12 @@ def tile_lineartransformerblock_pa_t_kernel(tc, x, cos, sin, Wq_words, Wq_scales
         xt_pool = ctx.enter_context(tc.psum_pool(name="xt", bufs=2))
         y_pool = ctx.enter_context(tc.psum_pool(name="y", bufs=4))
         bt_pool = ctx.enter_context(tc.psum_pool(name="bt", bufs=2))
+
+        zeros = consts.tile([P, UNIT_TOKENS], BF16)
+        nc.vector.memset(zeros[:], 0.0)
+        unread = bt_pool.tile([P, UNIT_TOKENS], F32, tag="bt")
+        for k in range(WARM_UP_MATMULS):
+            nc.tensor.matmul(out=unread[:], lhsT=zeros[:, 0:P], rhs=zeros[:], start=True, stop=True)
 
         def load_x(u):
             b, r = units[u]
@@ -159,20 +167,25 @@ def tile_lineartransformerblock_pa_t_kernel(tc, x, cos, sin, Wq_words, Wq_scales
                 y_heads.append(y)
             y_of[u] = y_heads
 
+        def pieces_of(u, h):
+            return LAST_PIECES if (u, h) == (len(units) - 1, HEADS - 1) else 1
+
         def multiply_by_tables(u):
             r = units[u][1]
             mine = slice(r * UNIT_TOKENS, (r + 1) * UNIT_TOKENS)
             prods = []
             for h, y in enumerate(y_of[u]):
                 prod = prod_pool.tile([P, 2, UNIT_TOKENS], F32)
-                nc.vector.scalar_tensor_tensor(
-                    out=prod[:],
-                    in0=y[:].unsqueeze(1).to_broadcast([P, 2, UNIT_TOKENS]),
-                    scalar=bias[:, h : h + 1],
-                    in1=tables[:, :, mine],
-                    op0=mybir.AluOpType.add,
-                    op1=mybir.AluOpType.mult,
-                )
+                width = UNIT_TOKENS // pieces_of(u, h)
+                for first in range(0, UNIT_TOKENS, width):
+                    nc.vector.scalar_tensor_tensor(
+                        out=prod[:, :, first : first + width],
+                        in0=y[:, first : first + width].unsqueeze(1).to_broadcast([P, 2, width]),
+                        scalar=bias[:, h : h + 1],
+                        in1=tables[:, :, mine.start + first : mine.start + first + width],
+                        op0=mybir.AluOpType.add,
+                        op1=mybir.AluOpType.mult,
+                    )
                 prods.append(prod)
             prod_of[u] = prods
 
@@ -180,23 +193,30 @@ def tile_lineartransformerblock_pa_t_kernel(tc, x, cos, sin, Wq_words, Wq_scales
             b, r = units[u]
             run = UNIT_TILES * HEAD_DIM
             prod = prod_of[u][h]
-            bt = bt_pool.tile([P, run], F32)
-            for i in range(UNIT_TILES):
-                cols = slice(i * P, (i + 1) * P)
-                nc.tensor.matmul(
-                    out=bt[:, cols], lhsT=prod[:, 0, cols], rhs=identity[:], is_transpose=True, start=True, stop=False
-                )
-                nc.tensor.matmul(
-                    out=bt[:, cols],
-                    lhsT=prod[:, 1, cols],
-                    rhs=swap[:].rearrange("p i j -> p (i j)"),
-                    is_transpose=True,
-                    start=False,
-                    stop=True,
-                )
-            result = out_pool.tile([P, run], F32)
-            nc.scalar.activation(out=result[:], in_=bt[:], func=mybir.ActivationFunctionType.Relu)
-            nc.sync.dma_start(out=out_view[b, :, h, r * run : (r + 1) * run], in_=result[:])
+            piece_tiles = UNIT_TILES // pieces_of(u, h)
+            for first_tile in range(0, UNIT_TILES, piece_tiles):
+                if pieces_of(u, h) == 1:
+                    bt = bt_pool.tile([P, piece_tiles * HEAD_DIM], F32)
+                else:
+                    bt = xt_pool.tile([P, piece_tiles * HEAD_DIM], F32, tag="xt")
+                for i in range(piece_tiles):
+                    tokens = slice((first_tile + i) * P, (first_tile + i + 1) * P)
+                    cols = slice(i * HEAD_DIM, (i + 1) * HEAD_DIM)
+                    nc.tensor.matmul(
+                        out=bt[:, cols], lhsT=prod[:, 0, tokens], rhs=identity[:], is_transpose=True, start=True, stop=False
+                    )
+                    nc.tensor.matmul(
+                        out=bt[:, cols],
+                        lhsT=prod[:, 1, tokens],
+                        rhs=swap[:].rearrange("p i j -> p (i j)"),
+                        is_transpose=True,
+                        start=False,
+                        stop=True,
+                    )
+                result = out_pool.tile([P, piece_tiles * HEAD_DIM], F32)
+                nc.scalar.activation(out=result[:], in_=bt[:], func=mybir.ActivationFunctionType.Relu)
+                first_col = r * run + first_tile * HEAD_DIM
+                nc.sync.dma_start(out=out_view[b, :, h, first_col : first_col + piece_tiles * HEAD_DIM], in_=result[:])
 
         for bank in range(UNIT_BANKS):
             transpose_and_regroup(0, bank)

@@ -25,6 +25,7 @@ WORDS = K // 2
 SORTED_BANK = 1
 FIRST_SORTED_UNIT = 3
 WARM_UP_MATMULS = 5
+GPSIMD_PIECES = 2
 LAST_PIECES = 2
 
 FLOPS = 2 * BATCH * TOKENS * K * HEADS * HEAD_DIM
@@ -170,11 +171,34 @@ def tile_lineartransformerblock_pa_t_kernel(tc, x, cos, sin, Wq_words, Wq_scales
         def pieces_of(u, h):
             return LAST_PIECES if (u, h) == (len(units) - 1, HEADS - 1) else 1
 
+        gpsimd_head = (len(units) - 2, HEADS - 1)
+
+        def multiply_by_tables_on_gpsimd():
+            u, h = gpsimd_head
+            mine = units[u][1] * UNIT_TOKENS
+            shifted = consts.tile([P, UNIT_TOKENS], F32)
+            nc.scalar.activation(
+                out=shifted[:], in_=y_of[u][h][:], func=mybir.ActivationFunctionType.Identity, bias=bias[:, h : h + 1]
+            )
+            prod = prod_pool.tile([P, 2, UNIT_TOKENS], F32)
+            width = UNIT_TOKENS // GPSIMD_PIECES
+            for first in range(0, UNIT_TOKENS, width):
+                nc.gpsimd.tensor_tensor(
+                    out=prod[:, :, first : first + width],
+                    in0=shifted[:, first : first + width].unsqueeze(1).to_broadcast([P, 2, width]),
+                    in1=tables[:, :, mine + first : mine + first + width],
+                    op=mybir.AluOpType.mult,
+                )
+            return prod
+
         def multiply_by_tables(u):
             r = units[u][1]
             mine = slice(r * UNIT_TOKENS, (r + 1) * UNIT_TOKENS)
             prods = []
             for h, y in enumerate(y_of[u]):
+                if (u, h) == gpsimd_head:
+                    prods.append(gpsimd_prod[0])
+                    continue
                 prod = prod_pool.tile([P, 2, UNIT_TOKENS], F32)
                 width = UNIT_TOKENS // pieces_of(u, h)
                 for first in range(0, UNIT_TOKENS, width):
@@ -239,7 +263,10 @@ def tile_lineartransformerblock_pa_t_kernel(tc, x, cos, sin, Wq_words, Wq_scales
         def in_range(u):
             return 0 <= u < len(units)
 
+        gpsimd_prod = []
         for step in range(1, len(units) + 4):
+            if step - 2 == gpsimd_head[0]:
+                gpsimd_prod.append(multiply_by_tables_on_gpsimd())
             for half_step in range(2):
                 if half_step == 1 and in_range(step + 1) and step + 1 >= FIRST_SORTED_UNIT:
                     sort_words(step + 1)

@@ -189,34 +189,28 @@ def tile_lineartransformerblock_pa_t_kernel(tc, x, cos, sin, Wq_words, Wq_scales
                     in1=tables[:, :, mine + first : mine + first + width],
                     op=mybir.AluOpType.mult,
                 )
-            return prod
+            prod_of[(u, h)] = prod
 
-        def multiply_by_tables(u):
-            r = units[u][1]
-            mine = slice(r * UNIT_TOKENS, (r + 1) * UNIT_TOKENS)
-            prods = []
-            for h, y in enumerate(y_of[u]):
-                if (u, h) == gpsimd_head:
-                    prods.append(gpsimd_prod[0])
-                    continue
-                prod = prod_pool.tile([P, 2, UNIT_TOKENS], F32)
-                width = UNIT_TOKENS // pieces_of(u, h)
-                for first in range(0, UNIT_TOKENS, width):
-                    nc.vector.scalar_tensor_tensor(
-                        out=prod[:, :, first : first + width],
-                        in0=y[:, first : first + width].unsqueeze(1).to_broadcast([P, 2, width]),
-                        scalar=bias[:, h : h + 1],
-                        in1=tables[:, :, mine.start + first : mine.start + first + width],
-                        op0=mybir.AluOpType.add,
-                        op1=mybir.AluOpType.mult,
-                    )
-                prods.append(prod)
-            prod_of[u] = prods
+        def multiply_by_tables(u, h):
+            mine = units[u][1] * UNIT_TOKENS
+            y = y_of[u][h]
+            prod = prod_pool.tile([P, 2, UNIT_TOKENS], F32)
+            width = UNIT_TOKENS // pieces_of(u, h)
+            for first in range(0, UNIT_TOKENS, width):
+                nc.vector.scalar_tensor_tensor(
+                    out=prod[:, :, first : first + width],
+                    in0=y[:, first : first + width].unsqueeze(1).to_broadcast([P, 2, width]),
+                    scalar=bias[:, h : h + 1],
+                    in1=tables[:, :, mine + first : mine + first + width],
+                    op0=mybir.AluOpType.add,
+                    op1=mybir.AluOpType.mult,
+                )
+            prod_of[(u, h)] = prod
 
         def turn_back_relu_store(u, h):
             b, r = units[u]
             run = UNIT_TILES * HEAD_DIM
-            prod = prod_of[u][h]
+            prod = prod_of[(u, h)]
             piece_tiles = UNIT_TILES // pieces_of(u, h)
             for first_tile in range(0, UNIT_TILES, piece_tiles):
                 if pieces_of(u, h) == 1:
@@ -263,10 +257,9 @@ def tile_lineartransformerblock_pa_t_kernel(tc, x, cos, sin, Wq_words, Wq_scales
         def in_range(u):
             return 0 <= u < len(units)
 
-        gpsimd_prod = []
         for step in range(1, len(units) + 4):
             if step - 2 == gpsimd_head[0]:
-                gpsimd_prod.append(multiply_by_tables_on_gpsimd())
+                multiply_by_tables_on_gpsimd()
             for half_step in range(2):
                 if half_step == 1 and in_range(step + 1) and step + 1 >= FIRST_SORTED_UNIT:
                     sort_words(step + 1)
@@ -274,9 +267,14 @@ def tile_lineartransformerblock_pa_t_kernel(tc, x, cos, sin, Wq_words, Wq_scales
                     transpose_and_regroup(step, half_step)
                 if in_range(step - 3):
                     turn_back_relu_store(step - 3, half_step)
+            if step == 2:
+                multiply_by_tables(0, 0)
+                quantise(1)
             if in_range(step - 1):
                 multiply(step - 1)
             if in_range(step - 2):
-                multiply_by_tables(step - 2)
-            if in_range(step):
+                for h in range(HEADS):
+                    if (step - 2, h) != gpsimd_head and (step, h) != (2, 0):
+                        multiply_by_tables(step - 2, h)
+            if in_range(step) and step != 1:
                 quantise(step)

@@ -23,7 +23,7 @@ UNIT_BANKS = UNIT_TILES // BANK_TILES
 UNIT_TOKENS = UNIT_TILES * P
 WORDS = K // 2
 SORTED_BANK = 1
-FIRST_SORTED_UNIT = 3
+FIRST_SORTED_UNIT = 5
 WARM_UP_MATMULS = 5
 GPSIMD_PIECES = 2
 LAST_PIECES = 2
@@ -46,13 +46,12 @@ def tile_lineartransformerblock_pa_t_kernel(tc, x, cos, sin, Wq_words, Wq_scales
         prod_pool = ctx.enter_context(tc.tile_pool(name="prod", bufs=6))
         out_pool = ctx.enter_context(tc.tile_pool(name="out", bufs=8))
         sorted_pool = ctx.enter_context(tc.tile_pool(name="sorted", bufs=3))
-        xt_pool = ctx.enter_context(tc.psum_pool(name="xt", bufs=2))
+        turn_pool = ctx.enter_context(tc.psum_pool(name="turn", bufs=4))
         y_pool = ctx.enter_context(tc.psum_pool(name="y", bufs=4))
-        bt_pool = ctx.enter_context(tc.psum_pool(name="bt", bufs=2))
 
         zeros = consts.tile([P, UNIT_TOKENS], BF16)
         nc.vector.memset(zeros[:], 0.0)
-        unread = bt_pool.tile([P, UNIT_TOKENS], F32, tag="bt")
+        unread = turn_pool.tile([P, UNIT_TOKENS], F32, tag="turn")
         for k in range(WARM_UP_MATMULS):
             nc.tensor.matmul(out=unread[:], lhsT=zeros[:, 0:P], rhs=zeros[:], start=True, stop=True)
 
@@ -132,7 +131,7 @@ def tile_lineartransformerblock_pa_t_kernel(tc, x, cos, sin, Wq_words, Wq_scales
                 grouped_of[u] = grouped
             grouped_words = grouped_of[u][:].bitcast(F32).rearrange("p (c half) -> p c half", half=2)
             x_words = x_tiles[u][bank][:].bitcast(F32)
-            xt = xt_pool.tile([P, 2, BANK_TILES * P], F32)
+            xt = turn_pool.tile([P, 2, BANK_TILES * P], F32, tag="turn")
             for i in range(BANK_TILES):
                 for half in range(2):
                     if bank == SORTED_BANK and u in sorted_of:
@@ -213,10 +212,7 @@ def tile_lineartransformerblock_pa_t_kernel(tc, x, cos, sin, Wq_words, Wq_scales
             prod = prod_of[(u, h)]
             piece_tiles = UNIT_TILES // pieces_of(u, h)
             for first_tile in range(0, UNIT_TILES, piece_tiles):
-                if pieces_of(u, h) == 1:
-                    bt = bt_pool.tile([P, piece_tiles * HEAD_DIM], F32)
-                else:
-                    bt = xt_pool.tile([P, piece_tiles * HEAD_DIM], F32, tag="xt")
+                bt = turn_pool.tile([P, piece_tiles * HEAD_DIM], F32, tag="turn")
                 for i in range(piece_tiles):
                     tokens = slice((first_tile + i) * P, (first_tile + i + 1) * P)
                     cols = slice(i * HEAD_DIM, (i + 1) * HEAD_DIM)
@@ -242,39 +238,47 @@ def tile_lineartransformerblock_pa_t_kernel(tc, x, cos, sin, Wq_words, Wq_scales
         tables = consts.tile([P, 2, TOKENS], BF16)
         turned_tables = []
         for raw in (cos_raw, partner_sin):
-            turned = y_pool.tile([P, TOKENS], BF16, tag="y")
+            turned = turn_pool.tile([P, TOKENS], BF16, tag="turn")
             for t in range(TOKENS_PER_PARTITION):
                 nc.tensor.transpose(out=turned[:, t * P : (t + 1) * P], in_=raw[:, t, :], identity=identity_bf[:])
             turned_tables.append(turned)
         bias_turned = y_pool.tile([P, P], BF16, tag="y")
         nc.tensor.transpose(out=bias_turned[:], in_=bias_rows[:], identity=identity_bf[:])
+        nc.scalar.copy(out=tables[:, 0, :], in_=turned_tables[0][:])
         quantise(0)
-        for which, turned in enumerate(turned_tables):
-            nc.vector.tensor_copy(out=tables[:, which, :], in_=turned[:])
+        nc.vector.tensor_copy(out=tables[:, 1, :], in_=turned_tables[1][:])
         bias = consts.tile([P, HEADS], F32)
         nc.vector.tensor_copy(out=bias[:], in_=bias_turned[:, 0:HEADS])
 
         def in_range(u):
             return 0 <= u < len(units)
 
-        for step in range(1, len(units) + 4):
+        for bank in range(UNIT_BANKS):
+            transpose_and_regroup(1, bank)
+        multiply(0)
+        multiply_by_tables(0, 0)
+        quantise(1)
+        multiply_by_tables(0, 1)
+        for u in (2, 3):
+            for bank in range(UNIT_BANKS):
+                transpose_and_regroup(u, bank)
+        multiply(1)
+        quantise(2)
+
+        for step in range(3, len(units) + 3):
             if step - 2 == gpsimd_head[0]:
                 multiply_by_tables_on_gpsimd()
             for half_step in range(2):
-                if half_step == 1 and in_range(step + 1) and step + 1 >= FIRST_SORTED_UNIT:
-                    sort_words(step + 1)
-                if in_range(step):
-                    transpose_and_regroup(step, half_step)
-                if in_range(step - 3):
-                    turn_back_relu_store(step - 3, half_step)
-            if step == 2:
-                multiply_by_tables(0, 0)
-                quantise(1)
+                if half_step == 1 and in_range(step + 2) and step + 2 >= FIRST_SORTED_UNIT:
+                    sort_words(step + 2)
+                if in_range(step + 1):
+                    transpose_and_regroup(step + 1, half_step)
+                turn_back_relu_store(step - 3, half_step)
             if in_range(step - 1):
                 multiply(step - 1)
             if in_range(step - 2):
                 for h in range(HEADS):
-                    if (step - 2, h) != gpsimd_head and (step, h) != (2, 0):
+                    if (step - 2, h) != gpsimd_head:
                         multiply_by_tables(step - 2, h)
-            if in_range(step) and step != 1:
+            if in_range(step):
                 quantise(step)

@@ -25,6 +25,7 @@ WORDS = K // 2
 SORTED_BANK = 1
 FIRST_SORTED_UNIT = 5
 WARM_UP_MATMULS = 5
+GPSIMD_UNITS = (1, 12, 14)
 GPSIMD_PIECES = 2
 LAST_PIECES = 2
 
@@ -43,11 +44,11 @@ def tile_lineartransformerblock_pa_t_kernel(tc, x, cos, sin, Wq_words, Wq_scales
         consts = ctx.enter_context(tc.tile_pool(name="consts", bufs=1))
         x_pool = ctx.enter_context(tc.tile_pool(name="x", bufs=len(units) * UNIT_BANKS))
         work = ctx.enter_context(tc.tile_pool(name="work", bufs=4))
-        prod_pool = ctx.enter_context(tc.tile_pool(name="prod", bufs=6))
+        prod_pool = ctx.enter_context(tc.tile_pool(name="prod", bufs=8))
         out_pool = ctx.enter_context(tc.tile_pool(name="out", bufs=8))
         sorted_pool = ctx.enter_context(tc.tile_pool(name="sorted", bufs=3))
-        turn_pool = ctx.enter_context(tc.psum_pool(name="turn", bufs=4))
-        y_pool = ctx.enter_context(tc.psum_pool(name="y", bufs=4))
+        turn_pool = ctx.enter_context(tc.psum_pool(name="turn", bufs=5))
+        y_pool = ctx.enter_context(tc.psum_pool(name="y", bufs=3))
 
         zeros = consts.tile([P, UNIT_TOKENS], BF16)
         nc.vector.memset(zeros[:], 0.0)
@@ -170,12 +171,12 @@ def tile_lineartransformerblock_pa_t_kernel(tc, x, cos, sin, Wq_words, Wq_scales
         def pieces_of(u, h):
             return LAST_PIECES if (u, h) == (len(units) - 1, HEADS - 1) else 1
 
-        gpsimd_head = (len(units) - 2, HEADS - 1)
+        def on_gpsimd(u, h):
+            return u in GPSIMD_UNITS and h == HEADS - 1
 
-        def multiply_by_tables_on_gpsimd():
-            u, h = gpsimd_head
+        def multiply_by_tables_on_gpsimd(u, h):
             mine = units[u][1] * UNIT_TOKENS
-            shifted = consts.tile([P, UNIT_TOKENS], F32)
+            shifted = work.tile([P, UNIT_TOKENS], F32)
             nc.scalar.activation(
                 out=shifted[:], in_=y_of[u][h][:], func=mybir.ActivationFunctionType.Identity, bias=bias[:, h : h + 1]
             )
@@ -266,19 +267,22 @@ def tile_lineartransformerblock_pa_t_kernel(tc, x, cos, sin, Wq_words, Wq_scales
         quantise(2)
 
         for step in range(3, len(units) + 3):
-            if step - 2 == gpsimd_head[0]:
-                multiply_by_tables_on_gpsimd()
+            if on_gpsimd(step - 2, HEADS - 1):
+                multiply_by_tables_on_gpsimd(step - 2, HEADS - 1)
             for half_step in range(2):
                 if half_step == 1 and in_range(step + 2) and step + 2 >= FIRST_SORTED_UNIT:
                     sort_words(step + 2)
                 if in_range(step + 1):
                     transpose_and_regroup(step + 1, half_step)
-                turn_back_relu_store(step - 3, half_step)
+                if half_step == 0 and on_gpsimd(step - 4, HEADS - 1):
+                    turn_back_relu_store(step - 4, HEADS - 1)
+                if not on_gpsimd(step - 3, half_step):
+                    turn_back_relu_store(step - 3, half_step)
             if in_range(step - 1):
                 multiply(step - 1)
             if in_range(step - 2):
                 for h in range(HEADS):
-                    if (step - 2, h) != gpsimd_head:
+                    if not on_gpsimd(step - 2, h):
                         multiply_by_tables(step - 2, h)
             if in_range(step):
                 quantise(step)

@@ -151,22 +151,19 @@ def tile_lineartransformerblock_pa_t_kernel(tc, x, cos, sin, Wq_words, Wq_scales
             nc.vector.quantize_mx(out=codes[:].bitcast(FP8X4), scales=scales[:], in_=grouped_of[u][:])
             codes_of[u] = (codes, scales)
 
-        def multiply(u):
+        def multiply(u, h):
             codes, scales = codes_of[u]
-            y_heads = []
-            for h in range(HEADS):
-                y = y_pool.tile([P, UNIT_TOKENS], F32)
-                nc.tensor.matmul_mx(
-                    out=y[:],
-                    lhsT=w_words[:, 2 * h * HEAD_DIM : 2 * (h + 1) * HEAD_DIM].bitcast(FP4X4),
-                    lhsT_scale=w_scales[:, h * HEAD_DIM : (h + 1) * HEAD_DIM],
-                    rhs=codes[:].bitcast(FP8X4),
-                    rhs_scale=scales[:],
-                    start=True,
-                    stop=True,
-                )
-                y_heads.append(y)
-            y_of[u] = y_heads
+            y = y_pool.tile([P, UNIT_TOKENS], F32)
+            nc.tensor.matmul_mx(
+                out=y[:],
+                lhsT=w_words[:, 2 * h * HEAD_DIM : 2 * (h + 1) * HEAD_DIM].bitcast(FP4X4),
+                lhsT_scale=w_scales[:, h * HEAD_DIM : (h + 1) * HEAD_DIM],
+                rhs=codes[:].bitcast(FP8X4),
+                rhs_scale=scales[:],
+                start=True,
+                stop=True,
+            )
+            y_of[(u, h)] = y
 
         def pieces_of(u, h):
             return LAST_PIECES if (u, h) == (len(units) - 1, HEADS - 1) else 1
@@ -178,7 +175,7 @@ def tile_lineartransformerblock_pa_t_kernel(tc, x, cos, sin, Wq_words, Wq_scales
             mine = units[u][1] * UNIT_TOKENS
             shifted = work.tile([P, UNIT_TOKENS], F32)
             nc.scalar.activation(
-                out=shifted[:], in_=y_of[u][h][:], func=mybir.ActivationFunctionType.Identity, bias=bias[:, h : h + 1]
+                out=shifted[:], in_=y_of[(u, h)][:], func=mybir.ActivationFunctionType.Identity, bias=bias[:, h : h + 1]
             )
             prod = prod_pool.tile([P, 2, UNIT_TOKENS], F32)
             width = UNIT_TOKENS // GPSIMD_PIECES
@@ -193,7 +190,7 @@ def tile_lineartransformerblock_pa_t_kernel(tc, x, cos, sin, Wq_words, Wq_scales
 
         def multiply_by_tables(u, h):
             mine = units[u][1] * UNIT_TOKENS
-            y = y_of[u][h]
+            y = y_of[(u, h)]
             prod = prod_pool.tile([P, 2, UNIT_TOKENS], F32)
             width = UNIT_TOKENS // pieces_of(u, h)
             for first in range(0, UNIT_TOKENS, width):
@@ -256,14 +253,16 @@ def tile_lineartransformerblock_pa_t_kernel(tc, x, cos, sin, Wq_words, Wq_scales
 
         for bank in range(UNIT_BANKS):
             transpose_and_regroup(1, bank)
-        multiply(0)
+        for h in range(HEADS):
+            multiply(0, h)
         multiply_by_tables(0, 0)
         quantise(1)
         multiply_by_tables(0, 1)
         for u in (2, 3):
             for bank in range(UNIT_BANKS):
                 transpose_and_regroup(u, bank)
-        multiply(1)
+        for h in range(HEADS):
+            multiply(1, h)
         quantise(2)
 
         for step in range(3, len(units) + 3):
@@ -278,8 +277,8 @@ def tile_lineartransformerblock_pa_t_kernel(tc, x, cos, sin, Wq_words, Wq_scales
                     turn_back_relu_store(step - 4, HEADS - 1)
                 if not on_gpsimd(step - 3, half_step):
                     turn_back_relu_store(step - 3, half_step)
-            if in_range(step - 1):
-                multiply(step - 1)
+                if in_range(step - 1):
+                    multiply(step - 1, half_step)
             if in_range(step - 2):
                 for h in range(HEADS):
                     if not on_gpsimd(step - 2, h):

from contextlib import ExitStack

import concourse.mybir as mybir
from concourse.masks import make_identity

F32 = mybir.dt.float32
BF16 = mybir.dt.bfloat16
I32 = mybir.dt.int32
U32 = mybir.dt.uint32
U8 = mybir.dt.uint8
FP8X4 = mybir.dt.float8_e4m3fn_x4
FP4X4 = mybir.dt.float4_e2m1fn_x4

P = 128
BATCH, TOKENS, K = 8, 1024, 512
HEADS, HEAD_DIM = 2, 128
PAIRS = HEAD_DIM // 2
TOKENS_PER_PARTITION = TOKENS // P
UNIT_TILES = 4
UNITS_PER_BATCH = TOKENS_PER_PARTITION // UNIT_TILES
BANK_TILES = 2
UNIT_BANKS = UNIT_TILES // BANK_TILES
UNIT_TOKENS = UNIT_TILES * P
WORDS = K // 2
SORTED_BANK = 1
FIRST_SORTED_UNIT = 5
WARM_UP_MATMULS = 5
GPSIMD_UNITS = (1, 12, 14)
GPSIMD_PIECES = 2
LAST_PIECES = 2

FLOPS = 2 * BATCH * TOKENS * K * HEADS * HEAD_DIM


def tile_lineartransformerblock_pa_t_kernel(tc, x, cos, sin, Wq_words, Wq_scales, bq, out):
    nc = tc.nc
    units = [(b, r) for b in range(BATCH) for r in range(UNITS_PER_BATCH)]

    x_view = x.rearrange("b (p t) k -> b p t k", t=TOKENS_PER_PARTITION)
    out_view = out.rearrange("b h (p t) d -> b p h (t d)", t=TOKENS_PER_PARTITION)

    with ExitStack() as ctx:
        ctx.enter_context(tc.manual_schedule())
        consts = ctx.enter_context(tc.tile_pool(name="consts", bufs=1))
        x_pool = ctx.enter_context(tc.tile_pool(name="x", bufs=len(units) * UNIT_BANKS))
        work = ctx.enter_context(tc.tile_pool(name="work", bufs=4))
        prod_pool = ctx.enter_context(tc.tile_pool(name="prod", bufs=8))
        out_pool = ctx.enter_context(tc.tile_pool(name="out", bufs=8))
        sorted_pool = ctx.enter_context(tc.tile_pool(name="sorted", bufs=3))
        turn_pool = ctx.enter_context(tc.psum_pool(name="turn", bufs=5))
        y_pool = ctx.enter_context(tc.psum_pool(name="y", bufs=3))

        zeros = consts.tile([P, UNIT_TOKENS], BF16)
        nc.vector.memset(zeros[:], 0.0)
        unread = turn_pool.tile([P, UNIT_TOKENS], F32, tag="turn")
        for k in range(WARM_UP_MATMULS):
            nc.tensor.matmul(out=unread[:], lhsT=zeros[:, 0:P], rhs=zeros[:], start=True, stop=True)

        def load_x(u):
            b, r = units[u]
            pieces = []
            for bank in range(UNIT_BANKS):
                first = r * UNIT_TILES + bank * BANK_TILES
                x_sb = x_pool.tile([P, BANK_TILES, K], BF16)
                nc.sync.dma_start(out=x_sb[:], in_=x_view[b, :, first : first + BANK_TILES, :])
                pieces.append(x_sb)
            return pieces

        x_tiles = [load_x(0)]

        cos_raw = consts.tile([P, TOKENS_PER_PARTITION, HEAD_DIM], BF16)
        sin_raw = consts.tile([P, TOKENS_PER_PARTITION, HEAD_DIM], BF16)
        for raw, table in ((sin_raw, sin), (cos_raw, cos)):
            nc.sync.dma_start(out=raw[:], in_=table.rearrange("(p t) d -> p t d", t=TOKENS_PER_PARTITION))

        x_tiles.append(load_x(1))

        w_words = consts.tile([P, 2 * HEADS * HEAD_DIM], U8, align_bytes=64)
        nc.sync.dma_start(out=w_words[:].bitcast(I32), in_=Wq_words[0].bitcast(I32))
        w_scales = consts.tile([P, HEADS * HEAD_DIM], U8, align_bytes=64)
        nc.vector.memset(w_scales[:].bitcast(I32), 0)
        for quadrant in range(4):
            nc.sync.dma_start(
                out=w_scales[32 * quadrant : 32 * quadrant + 4, :].bitcast(I32),
                in_=Wq_scales[0, 4 * quadrant : 4 * quadrant + 4, :].bitcast(I32),
            )
        for u in range(2, len(units)):
            x_tiles.append(load_x(u))

        identity = consts.tile([P, P], F32)
        make_identity(nc, identity[:])
        identity_bf = consts.tile([P, P], BF16)
        make_identity(nc, identity_bf[:])
        swap = consts.tile([P, PAIRS, 2], F32)
        identity_pairs = identity[:].rearrange("p (i j) -> p i j", j=2)
        for j in range(2):
            nc.gpsimd.tensor_copy(out=swap[:, :, j], in_=identity_pairs[:, :, 1 - j])

        table_warmer = consts.tile([P, 1], F32)
        nc.vector.memset(table_warmer[:], 0.0)
        nc.scalar.activation(out=table_warmer[:], in_=table_warmer[:], func=mybir.ActivationFunctionType.Relu)

        bias_rows = consts.tile([P, HEAD_DIM], BF16)
        nc.vector.memset(bias_rows[:], 0.0)
        nc.scalar.dma_start(out=bias_rows[0:HEADS, :], in_=bq.rearrange("(h d) -> h d", h=HEADS))

        partner_sin = consts.tile([P, TOKENS_PER_PARTITION, HEAD_DIM], BF16)
        for j in range(2):
            nc.vector.tensor_scalar(
                out=partner_sin[:, :, j:HEAD_DIM:2],
                in0=sin_raw[:, :, 1 - j : HEAD_DIM : 2],
                scalar1=1.0 - 2.0 * j,
                scalar2=None,
                op0=mybir.AluOpType.mult,
            )

        grouped_of, codes_of, y_of, prod_of = {}, {}, {}, {}

        sorted_of = {}

        def sort_words(u):
            x_sorted = sorted_pool.tile([P, BANK_TILES, 2, WORDS // 2], F32)
            nc.scalar.copy(
                out=x_sorted[:],
                in_=x_tiles[u][SORTED_BANK][:].bitcast(F32).rearrange("p i (w half) -> p i half w", half=2),
            )
            sorted_of[u] = x_sorted

        def transpose_and_regroup(u, bank):
            if bank == 0:
                grouped = work.tile([P, 4 * UNIT_TOKENS], BF16, align_bytes=64)
                grouped_of[u] = grouped
            grouped_words = grouped_of[u][:].bitcast(F32).rearrange("p (c half) -> p c half", half=2)
            x_words = x_tiles[u][bank][:].bitcast(F32)
            xt = turn_pool.tile([P, 2, BANK_TILES * P], F32, tag="turn")
            for i in range(BANK_TILES):
                for half in range(2):
                    if bank == SORTED_BANK and u in sorted_of:
                        words_in = sorted_of[u][:, i, half, :]
                    else:
                        words_in = x_words[:, i, half:WORDS:2]
                    nc.tensor.transpose(out=xt[:, half, i * P : (i + 1) * P], in_=words_in, identity=identity[:])
            nc.scalar.copy(
                out=grouped_words[:, bank * BANK_TILES * P : (bank + 1) * BANK_TILES * P, :],
                in_=xt[:].rearrange("p half c -> p c half"),
            )

        def quantise(u):
            codes = work.tile([P, UNIT_TOKENS], U32, align_bytes=64)
            scales = work.tile([P, UNIT_TOKENS], U8, align_bytes=64)
            nc.vector.quantize_mx(out=codes[:].bitcast(FP8X4), scales=scales[:], in_=grouped_of[u][:])
            codes_of[u] = (codes, scales)

        def multiply(u, h):
            codes, scales = codes_of[u]
            y = y_pool.tile([P, UNIT_TOKENS], F32)
            nc.tensor.matmul_mx(
                out=y[:],
                lhsT=w_words[:, 2 * h * HEAD_DIM : 2 * (h + 1) * HEAD_DIM].bitcast(FP4X4),
                lhsT_scale=w_scales[:, h * HEAD_DIM : (h + 1) * HEAD_DIM],
                rhs=codes[:].bitcast(FP8X4),
                rhs_scale=scales[:],
                start=True,
                stop=True,
            )
            y_of[(u, h)] = y

        def pieces_of(u, h):
            return LAST_PIECES if (u, h) == (len(units) - 1, HEADS - 1) else 1

        def on_gpsimd(u, h):
            return u in GPSIMD_UNITS and h == HEADS - 1

        def multiply_by_tables_on_gpsimd(u, h):
            mine = units[u][1] * UNIT_TOKENS
            shifted = work.tile([P, UNIT_TOKENS], F32)
            nc.scalar.activation(
                out=shifted[:], in_=y_of[(u, h)][:], func=mybir.ActivationFunctionType.Identity, bias=bias[:, h : h + 1]
            )
            prod = prod_pool.tile([P, 2, UNIT_TOKENS], F32)
            width = UNIT_TOKENS // GPSIMD_PIECES
            for first in range(0, UNIT_TOKENS, width):
                nc.gpsimd.tensor_tensor(
                    out=prod[:, :, first : first + width],
                    in0=shifted[:, first : first + width].unsqueeze(1).to_broadcast([P, 2, width]),
                    in1=tables[:, :, mine + first : mine + first + width],
                    op=mybir.AluOpType.mult,
                )
            prod_of[(u, h)] = prod

        def multiply_by_tables(u, h):
            mine = units[u][1] * UNIT_TOKENS
            y = y_of[(u, h)]
            prod = prod_pool.tile([P, 2, UNIT_TOKENS], F32)
            width = UNIT_TOKENS // pieces_of(u, h)
            for first in range(0, UNIT_TOKENS, width):
                nc.vector.scalar_tensor_tensor(
                    out=prod[:, :, first : first + width],
                    in0=y[:, first : first + width].unsqueeze(1).to_broadcast([P, 2, width]),
                    scalar=bias[:, h : h + 1],
                    in1=tables[:, :, mine + first : mine + first + width],
                    op0=mybir.AluOpType.add,
                    op1=mybir.AluOpType.mult,
                )
            prod_of[(u, h)] = prod

        def turn_back_relu_store(u, h):
            b, r = units[u]
            run = UNIT_TILES * HEAD_DIM
            prod = prod_of[(u, h)]
            piece_tiles = UNIT_TILES // pieces_of(u, h)
            for first_tile in range(0, UNIT_TILES, piece_tiles):
                bt = turn_pool.tile([P, piece_tiles * HEAD_DIM], F32, tag="turn")
                for i in range(piece_tiles):
                    tokens = slice((first_tile + i) * P, (first_tile + i + 1) * P)
                    cols = slice(i * HEAD_DIM, (i + 1) * HEAD_DIM)
                    nc.tensor.matmul(
                        out=bt[:, cols], lhsT=prod[:, 0, tokens], rhs=identity[:], is_transpose=True, start=True, stop=False
                    )
                    nc.tensor.matmul(
                        out=bt[:, cols],
                        lhsT=prod[:, 1, tokens],
                        rhs=swap[:].rearrange("p i j -> p (i j)"),
                        is_transpose=True,
                        start=False,
                        stop=True,
                    )
                result = out_pool.tile([P, piece_tiles * HEAD_DIM], F32)
                nc.scalar.activation(out=result[:], in_=bt[:], func=mybir.ActivationFunctionType.Relu)
                first_col = r * run + first_tile * HEAD_DIM
                nc.sync.dma_start(out=out_view[b, :, h, first_col : first_col + piece_tiles * HEAD_DIM], in_=result[:])

        for bank in range(UNIT_BANKS):
            transpose_and_regroup(0, bank)

        tables = consts.tile([P, 2, TOKENS], BF16)
        turned_tables = []
        for raw in (cos_raw, partner_sin):
            turned = turn_pool.tile([P, TOKENS], BF16, tag="turn")
            for t in range(TOKENS_PER_PARTITION):
                nc.tensor.transpose(out=turned[:, t * P : (t + 1) * P], in_=raw[:, t, :], identity=identity_bf[:])
            turned_tables.append(turned)
        bias_turned = y_pool.tile([P, P], BF16, tag="y")
        nc.tensor.transpose(out=bias_turned[:], in_=bias_rows[:], identity=identity_bf[:])
        nc.scalar.copy(out=tables[:, 0, :], in_=turned_tables[0][:])
        quantise(0)
        nc.vector.tensor_copy(out=tables[:, 1, :], in_=turned_tables[1][:])
        bias = consts.tile([P, HEADS], F32)
        nc.vector.tensor_copy(out=bias[:], in_=bias_turned[:, 0:HEADS])

        def in_range(u):
            return 0 <= u < len(units)

        for bank in range(UNIT_BANKS):
            transpose_and_regroup(1, bank)
        for h in range(HEADS):
            multiply(0, h)
        multiply_by_tables(0, 0)
        quantise(1)
        multiply_by_tables(0, 1)
        for u in (2, 3):
            for bank in range(UNIT_BANKS):
                transpose_and_regroup(u, bank)
        for h in range(HEADS):
            multiply(1, h)
        quantise(2)

        for step in range(3, len(units) + 3):
            if on_gpsimd(step - 2, HEADS - 1):
                multiply_by_tables_on_gpsimd(step - 2, HEADS - 1)
            for half_step in range(2):
                if half_step == 1 and in_range(step + 2) and step + 2 >= FIRST_SORTED_UNIT:
                    sort_words(step + 2)
                if in_range(step + 1):
                    transpose_and_regroup(step + 1, half_step)
                if half_step == 0 and on_gpsimd(step - 4, HEADS - 1):
                    turn_back_relu_store(step - 4, HEADS - 1)
                if not on_gpsimd(step - 3, half_step):
                    turn_back_relu_store(step - 3, half_step)
                if in_range(step - 1):
                    multiply(step - 1, half_step)
            if in_range(step - 2):
                for h in range(HEADS):
                    if not on_gpsimd(step - 2, h):
                        multiply_by_tables(step - 2, h)
            if in_range(step):
                quantise(step)
